import numpy as np
import ml_dtypes


def mxq(x, axis, fmt="e4m3"):
    dtype, down = {"e4m3": (ml_dtypes.float8_e4m3fn, 7), "e5m2": (ml_dtypes.float8_e5m2, 14)}[fmt]
    v = np.moveaxis(np.asarray(x, np.float32).astype(ml_dtypes.bfloat16).astype(np.float64), axis, -1)
    blocks = v.reshape(v.shape[:-1] + (-1, 32))
    amax = np.abs(blocks).max(-1, keepdims=True)
    byte = np.maximum(np.where(amax > 0, np.frexp(amax)[1] - 1 + 127, 0) - down, 1)
    scale = np.exp2(byte - 127.0)
    codes = (blocks / scale).astype(np.float32).astype(dtype).astype(np.float64)
    return np.moveaxis((codes * scale).reshape(v.shape), -1, axis)


WIDE = False


def mx_kscale(k):
    if not WIDE:
        return np.ones(k)
    levels = np.array([10, -10, 5, -5, 0])
    a = np.random.permutation(np.resize(levels, k // 512 * 4)).reshape(k // 512, 4)
    idx = np.arange(k)
    return np.exp2(a[idx // 512, idx % 128 // 32])


BF16 = ml_dtypes.bfloat16


def bf(x):
    return np.asarray(x, np.float32).astype(BF16)


def f64(x):
    return np.asarray(x).astype(np.float64)


B, S, DIM, HID, R, NT = 8, 64, 1024, 2560, 128, 3
SCALING = 4.0


def silu(v):
    return v / (1.0 + np.exp(-v))


def lora_out(xa, bw, tw):
    return (xa @ bw) * SCALING * tw[..., None]


def setup_inputs():
    s = mx_kscale(DIM)
    return {"x": bf(np.random.standard_normal((B, S, DIM)) * s),
            "w1": bf(np.random.standard_normal((DIM, HID)) / np.sqrt(DIM) / s[:, None]),
            "w3": bf(np.random.standard_normal((DIM, HID)) / np.sqrt(DIM) / s[:, None]),
            "xa_up": bf(np.random.standard_normal((B, S, R))),
            "b_up": bf(np.random.standard_normal((R, HID)) * 0.2 / np.sqrt(R)),
            "xa_gate": bf(np.random.standard_normal((B, S, R))),
            "b_gate": bf(np.random.standard_normal((R, HID)) * 0.2 / np.sqrt(R)),
            "tw_up": bf(np.random.uniform(size=(B, S))),
            "tw_gate": bf(np.random.uniform(size=(B, S)))}


def reference(x, w1, w3, xa_up, b_up, xa_gate, b_gate, tw_up, tw_gate):
    xq = mxq(f64(x), 2, "e4m3")
    up = (xq @ mxq(f64(w3), 0, "e4m3")) + lora_out(f64(xa_up), f64(b_up), f64(tw_up))
    gate = silu((xq @ mxq(f64(w1), 0, "e4m3")) + lora_out(f64(xa_gate), f64(b_gate), f64(tw_gate)))
    return gate * up

@@ -1,0 +1,195 @@
+from contextlib import ExitStack
+
+import concourse.mybir as mybir
+from concourse.masks import make_identity
+
+F32 = mybir.dt.float32
+BF16 = mybir.dt.bfloat16
+U32 = mybir.dt.uint32
+U8 = mybir.dt.uint8
+FP8X4 = mybir.dt.float8_e4m3fn_x4
+ACT = mybir.ActivationFunctionType
+ALU = mybir.AluOpType
+
+P = 128
+PACK = 4
+K_PASS = P * PACK
+TOKENS = 512
+DIM = 1024
+HID = 2560
+RANK = 128
+SCALING = 4.0
+T_TILES = TOKENS // P
+PASSES = DIM // K_PASS
+N_TILE = 512
+H_TILES = HID // N_TILE
+RUN = 4
+
+FLOPS = 2 * TOKENS * HID * 2 * (DIM + RANK)
+
+
+def load_weight_tile(nc, pool, w, h):
+    raw = pool.tile([P, PASSES, PACK, N_TILE], BF16, tag="w_raw")
+    for c in range(PASSES):
+        nc.sync.dma_start(
+            out=raw[:, c, :, :],
+            in_=w[c * K_PASS : (c + 1) * K_PASS, h * N_TILE : (h + 1) * N_TILE].rearrange(
+                "(p j) n -> p j n", j=PACK
+            ),
+        )
+    return raw
+
+
+def load_adapter_tile(nc, pool, b, h):
+    b_tile = pool.tile([P, N_TILE], BF16, tag="b_tile")
+    nc.sync.dma_start(out=b_tile[:], in_=b[:, h * N_TILE : (h + 1) * N_TILE])
+    return b_tile
+
+
+def quantise_weight_tile(nc, grouped_pool, mx_pool, raw):
+    grouped = grouped_pool.tile([P, PASSES, N_TILE, PACK], BF16, align_bytes=64)
+    nc.vector.tensor_copy(
+        out=grouped[:, 0].rearrange("p (g i) j -> p g j i", i=RUN),
+        in_=raw[:, 0].rearrange("p j (g i) -> p g j i", i=RUN),
+    )
+    nc.scalar.copy(
+        out=grouped[:, 1].rearrange("p (g i) j -> p g j i", i=RUN),
+        in_=raw[:, 1].rearrange("p j (g i) -> p g j i", i=RUN),
+    )
+    codes = mx_pool.tile([P, PASSES, N_TILE], U32, align_bytes=64)
+    scales = mx_pool.tile([P, PASSES, N_TILE], U8, align_bytes=64)
+    nc.vector.quantize_mx(
+        out=codes[:].rearrange("p c n -> p (c n)").bitcast(FP8X4),
+        scales=scales[:].rearrange("p c n -> p (c n)"),
+        in_=grouped[:].rearrange("p c n j -> p (c n j)"),
+    )
+    return codes, scales
+
+
+def tile_feedforward_pa_kernel(
+    tc, x, w1, w3, xa_up, b_up, xa_gate, b_gate, tw_up, tw_gate, out
+):
+    nc = tc.nc
+    x_rows = x.flatten_outer_dims()
+    out_rows = out.flatten_outer_dims()
+    sides = ("gate", "up")
+    weight = {"gate": w1, "up": w3}
+    xa = {"gate": xa_gate, "up": xa_up}
+    b = {"gate": b_gate, "up": b_up}
+    tw = {"gate": tw_gate, "up": tw_up}
+
+    with ExitStack() as ctx:
+        keep = ctx.enter_context(tc.tile_pool(name="keep", bufs=1))
+        raw_pool = ctx.enter_context(tc.tile_pool(name="raw", bufs=2 * H_TILES))
+        b_pool = ctx.enter_context(tc.tile_pool(name="adapter", bufs=2 * H_TILES))
+        grouped_pool = ctx.enter_context(tc.tile_pool(name="grouped", bufs=3))
+        mx_pool = ctx.enter_context(tc.tile_pool(name="mx", bufs=3))
+        work = ctx.enter_context(tc.tile_pool(name="work", bufs=3))
+        act_pool = ctx.enter_context(tc.tile_pool(name="act", bufs=2 * T_TILES))
+        psum = ctx.enter_context(tc.psum_pool(name="psum", bufs=4))
+
+        ident_bf16 = keep.tile([P, P], BF16)
+        make_identity(nc, ident_bf16[:])
+        ident_f32 = keep.tile([P, P], F32)
+        make_identity(nc, ident_f32[:])
+        tw_rows = keep.tile([P, P], BF16)
+        nc.gpsimd.memset(tw_rows[:], 0.0)
+
+        xa_raw = {}
+        for i, side in enumerate(sides):
+            xa_raw[side] = keep.tile([P, T_TILES, RANK], BF16, name="xa_raw_" + side)
+            nc.sync.dma_start(
+                out=xa_raw[side][:],
+                in_=xa[side].flatten_outer_dims().rearrange("(t p) r -> p t r", p=P),
+            )
+            nc.sync.dma_start(
+                out=tw_rows[i * T_TILES : (i + 1) * T_TILES, :],
+                in_=tw[side].rearrange("(t u) s -> t (u s)", t=T_TILES),
+            )
+        x_raw = keep.tile([P, T_TILES, DIM], BF16)
+        w_raw = {}
+        b_tile = {}
+        for h in range(H_TILES):
+            for side in sides:
+                w_raw[side, h] = load_weight_tile(nc, raw_pool, weight[side], h)
+                b_tile[side, h] = load_adapter_tile(nc, b_pool, b[side], h)
+                if h == 0 and side == "gate":
+                    for t in range(T_TILES):
+                        nc.sync.dma_start(out=x_raw[:, t, :], in_=x_rows[t * P : (t + 1) * P, :])
+
+        xa_t = {}
+        for side in sides:
+            xa_t_ps = psum.tile([P, T_TILES, P], BF16, tag="lora")
+            for t in range(T_TILES):
+                nc.tensor.transpose(out=xa_t_ps[:, t, :], in_=xa_raw[side][:, t, :], identity=ident_bf16[:])
+            xa_t[side] = keep.tile([P, T_TILES, P], BF16, name="xa_t_" + side)
+            nc.scalar.copy(out=xa_t[side][:], in_=xa_t_ps[:])
+        tw_ps = psum.tile([P, P], BF16, tag="lora")
+        nc.tensor.transpose(out=tw_ps[:], in_=tw_rows[:], identity=ident_bf16[:])
+        token_scale = keep.tile([P, 2 * T_TILES], F32)
+        nc.scalar.activation(
+            out=token_scale[:], in_=tw_ps[:, 0 : 2 * T_TILES], func=ACT.Copy, scale=SCALING
+        )
+
+        mx_w = {("gate", 0): quantise_weight_tile(nc, grouped_pool, mx_pool, w_raw["gate", 0])}
+
+        x_grouped = keep.tile([P, T_TILES, PASSES * P * PACK], BF16, align_bytes=64)
+        x_codes = keep.tile([P, T_TILES, PASSES, P], U32, align_bytes=64)
+        x_scales = keep.tile([P, T_TILES, PASSES, P], U8, align_bytes=64)
+        for t in range(T_TILES):
+            x_words = x_raw[:, t, :].bitcast(F32).rearrange("p (c q u) -> p c u q", c=PASSES, u=2)
+            x_t_ps = psum.tile([P, PASSES, 2, P], F32, tag="mx")
+            for c in range(PASSES):
+                for u in range(2):
+                    nc.tensor.transpose(out=x_t_ps[:, c, u, :], in_=x_words[:, c, u, :], identity=ident_f32[:])
+            grouped_words = x_grouped[:, t, :].bitcast(F32).rearrange("p (c m u) -> p c m u", c=PASSES, u=2)
+            if t % 2 == 0:
+                nc.vector.tensor_copy(out=grouped_words, in_=x_t_ps[:].rearrange("p c u m -> p c m u"))
+            else:
+                nc.scalar.copy(out=grouped_words, in_=x_t_ps[:].rearrange("p c u m -> p c m u"))
+        for t in range(T_TILES):
+            nc.vector.quantize_mx(
+                out=x_codes[:, t].rearrange("p c m -> p (c m)").bitcast(FP8X4),
+                scales=x_scales[:, t].rearrange("p c m -> p (c m)"),
+                in_=x_grouped[:, t, :],
+            )
+
+        def projection(side, h, t):
+            codes, scales = mx_w[side, h]
+            lora = psum.tile([P, N_TILE], F32, tag="lora")
+            nc.tensor.matmul(out=lora[:], lhsT=xa_t[side][:, t, :], rhs=b_tile[side, h][:], start=True, stop=True)
+            acc = psum.tile([P, N_TILE], F32, tag="mx")
+            for c in range(PASSES):
+                nc.tensor.matmul_mx(
+                    out=acc[:],
+                    lhsT=x_codes[:, t, c, :].bitcast(FP8X4),
+                    lhsT_scale=x_scales[:, t, c, :],
+                    rhs=codes[:, c, :].bitcast(FP8X4),
+                    rhs_scale=scales[:, c, :],
+                    start=(c == 0),
+                    stop=(c == PASSES - 1),
+                )
+            col = sides.index(side) * T_TILES + t
+            scaled = work.tile([P, N_TILE], F32, tag="scaled")
+            nc.scalar.activation(out=scaled[:], in_=lora[:], func=ACT.Copy, scale=token_scale[:, col : col + 1])
+            total = work.tile([P, N_TILE], F32, tag="total")
+            nc.vector.tensor_tensor(out=total[:], in0=acc[:], in1=scaled[:], op=ALU.add)
+            return total
+
+        for h in range(H_TILES):
+            mx_w["up", h] = quantise_weight_tile(nc, grouped_pool, mx_pool, w_raw["up", h])
+            gate_act = []
+            for t in range(T_TILES):
+                total = projection("gate", h, t)
+                act = act_pool.tile([P, N_TILE], F32, tag="act")
+                nc.scalar.activation(out=act[:], in_=total[:], func=ACT.Silu)
+                gate_act.append(act)
+            if h + 1 < H_TILES:
+                mx_w["gate", h + 1] = quantise_weight_tile(nc, grouped_pool, mx_pool, w_raw["gate", h + 1])
+            for t in range(T_TILES):
+                total = projection("up", h, t)
+                hidden = work.tile([P, N_TILE], F32, tag="hidden")
+                nc.vector.tensor_tensor(out=hidden[:], in0=gate_act[t][:], in1=total[:], op=ALU.mult)
+                nc.sync.dma_start(
+                    out=out_rows[t * P : (t + 1) * P, h * N_TILE : (h + 1) * N_TILE], in_=hidden[:]
+                )

@@ -23,47 +23,20 @@ T_TILES = TOKENS // P
 PASSES = DIM // K_PASS
 N_TILE = 512
 H_TILES = HID // N_TILE
+UNITS = H_TILES * T_TILES
 RUN = 4
+SCALAR_COLS = 320
+LEAD = 4
 
 FLOPS = 2 * TOKENS * HID * 2 * (DIM + RANK)
 
 
-def load_weight_tile(nc, pool, w, h):
-    raw = pool.tile([P, PASSES, PACK, N_TILE], BF16, tag="w_raw")
-    for c in range(PASSES):
-        nc.sync.dma_start(
-            out=raw[:, c, :, :],
-            in_=w[c * K_PASS : (c + 1) * K_PASS, h * N_TILE : (h + 1) * N_TILE].rearrange(
-                "(p j) n -> p j n", j=PACK
-            ),
-        )
-    return raw
+def regrouped(ap):
+    return ap.rearrange("p (g i) j -> p g j i", i=RUN)
 
 
-def load_adapter_tile(nc, pool, b, h):
-    b_tile = pool.tile([P, N_TILE], BF16, tag="b_tile")
-    nc.sync.dma_start(out=b_tile[:], in_=b[:, h * N_TILE : (h + 1) * N_TILE])
-    return b_tile
-
-
-def quantise_weight_tile(nc, grouped_pool, mx_pool, raw):
-    grouped = grouped_pool.tile([P, PASSES, N_TILE, PACK], BF16, align_bytes=64)
-    nc.vector.tensor_copy(
-        out=grouped[:, 0].rearrange("p (g i) j -> p g j i", i=RUN),
-        in_=raw[:, 0].rearrange("p j (g i) -> p g j i", i=RUN),
-    )
-    nc.scalar.copy(
-        out=grouped[:, 1].rearrange("p (g i) j -> p g j i", i=RUN),
-        in_=raw[:, 1].rearrange("p j (g i) -> p g j i", i=RUN),
-    )
-    codes = mx_pool.tile([P, PASSES, N_TILE], U32, align_bytes=64)
-    scales = mx_pool.tile([P, PASSES, N_TILE], U8, align_bytes=64)
-    nc.vector.quantize_mx(
-        out=codes[:].rearrange("p c n -> p (c n)").bitcast(FP8X4),
-        scales=scales[:].rearrange("p c n -> p (c n)"),
-        in_=grouped[:].rearrange("p c n j -> p (c n j)"),
-    )
-    return codes, scales
+def as_loaded(ap):
+    return ap.rearrange("p j (g i) -> p g j i", i=RUN)
 
 
 def tile_feedforward_pa_kernel(
@@ -82,11 +55,12 @@ def tile_feedforward_pa_kernel(
         keep = ctx.enter_context(tc.tile_pool(name="keep", bufs=1))
         raw_pool = ctx.enter_context(tc.tile_pool(name="raw", bufs=2 * H_TILES))
         b_pool = ctx.enter_context(tc.tile_pool(name="adapter", bufs=2 * H_TILES))
-        grouped_pool = ctx.enter_context(tc.tile_pool(name="grouped", bufs=3))
-        mx_pool = ctx.enter_context(tc.tile_pool(name="mx", bufs=3))
+        grouped_pool = ctx.enter_context(tc.tile_pool(name="grouped", bufs=2))
+        mx_pool = ctx.enter_context(tc.tile_pool(name="mx", bufs=4))
         work = ctx.enter_context(tc.tile_pool(name="work", bufs=3))
-        act_pool = ctx.enter_context(tc.tile_pool(name="act", bufs=2 * T_TILES))
+        out_pool = ctx.enter_context(tc.tile_pool(name="out", bufs=8))
         psum = ctx.enter_context(tc.psum_pool(name="psum", bufs=4))
+        ctx.enter_context(tc.manual_schedule())
 
         ident_bf16 = keep.tile([P, P], BF16)
         make_identity(nc, ident_bf16[:])
@@ -110,12 +84,22 @@ def tile_feedforward_pa_kernel(
         w_raw = {}
         b_tile = {}
         for h in range(H_TILES):
+            columns = slice(h * N_TILE, (h + 1) * N_TILE)
             for side in sides:
-                w_raw[side, h] = load_weight_tile(nc, raw_pool, weight[side], h)
-                b_tile[side, h] = load_adapter_tile(nc, b_pool, b[side], h)
-                if h == 0 and side == "gate":
-                    for t in range(T_TILES):
-                        nc.sync.dma_start(out=x_raw[:, t, :], in_=x_rows[t * P : (t + 1) * P, :])
+                b_tile[side, h] = b_pool.tile([P, N_TILE], BF16, name="b_tile")
+                nc.sync.dma_start(out=b_tile[side, h][:], in_=b[side][:, columns])
+            for side in sides:
+                w_raw[side, h] = raw_pool.tile([P, PASSES, PACK, N_TILE], BF16, name="w_raw")
+                for c in range(PASSES):
+                    nc.sync.dma_start(
+                        out=w_raw[side, h][:, c],
+                        in_=weight[side][c * K_PASS : (c + 1) * K_PASS, columns].rearrange(
+                            "(p j) n -> p j n", j=PACK
+                        ),
+                    )
+            if h == 0:
+                for t in range(T_TILES):
+                    nc.sync.dma_start(out=x_raw[:, t, :], in_=x_rows[t * P : (t + 1) * P, :])
 
         xa_t = {}
         for side in sides:
@@ -131,33 +115,71 @@ def tile_feedforward_pa_kernel(
             out=token_scale[:], in_=tw_ps[:, 0 : 2 * T_TILES], func=ACT.Copy, scale=SCALING
         )
 
-        mx_w = {("gate", 0): quantise_weight_tile(nc, grouped_pool, mx_pool, w_raw["gate", 0])}
+        grouped = {}
+        mx_w = {}
+
+        def prepare(half_step):
+            i = half_step // 2
+            if i >= 2 * H_TILES:
+                return
+            key = (sides[i % 2], i // 2)
+            if half_step % 2 == 0:
+                raw = w_raw[key]
+                grouped[key] = grouped_pool.tile([P, PASSES, N_TILE, PACK], BF16, name="grouped", align_bytes=64)
+                split = N_TILE - SCALAR_COLS
+                nc.scalar.copy(out=regrouped(grouped[key][:, 1, split:, :]), in_=as_loaded(raw[:, 1, :, split:]))
+                nc.vector.tensor_copy(out=regrouped(grouped[key][:, 0]), in_=as_loaded(raw[:, 0]))
+                nc.vector.tensor_copy(
+                    out=regrouped(grouped[key][:, 1, :split, :]), in_=as_loaded(raw[:, 1, :, :split])
+                )
+            else:
+                codes = mx_pool.tile([P, PASSES, N_TILE], U32, align_bytes=64)
+                scales = mx_pool.tile([P, PASSES, N_TILE], U8, align_bytes=64)
+                nc.vector.quantize_mx(
+                    out=codes[:].rearrange("p c n -> p (c n)").bitcast(FP8X4),
+                    scales=scales[:].rearrange("p c n -> p (c n)"),
+                    in_=grouped[key][:].rearrange("p c n j -> p (c n j)"),
+                )
+                mx_w[key] = (codes, scales)
 
         x_grouped = keep.tile([P, T_TILES, PASSES * P * PACK], BF16, align_bytes=64)
         x_codes = keep.tile([P, T_TILES, PASSES, P], U32, align_bytes=64)
         x_scales = keep.tile([P, T_TILES, PASSES, P], U8, align_bytes=64)
-        for t in range(T_TILES):
+
+        def transpose_x(t):
             x_words = x_raw[:, t, :].bitcast(F32).rearrange("p (c q u) -> p c u q", c=PASSES, u=2)
             x_t_ps = psum.tile([P, PASSES, 2, P], F32, tag="mx")
             for c in range(PASSES):
                 for u in range(2):
                     nc.tensor.transpose(out=x_t_ps[:, c, u, :], in_=x_words[:, c, u, :], identity=ident_f32[:])
             grouped_words = x_grouped[:, t, :].bitcast(F32).rearrange("p (c m u) -> p c m u", c=PASSES, u=2)
-            if t % 2 == 0:
-                nc.vector.tensor_copy(out=grouped_words, in_=x_t_ps[:].rearrange("p c u m -> p c m u"))
-            else:
-                nc.scalar.copy(out=grouped_words, in_=x_t_ps[:].rearrange("p c u m -> p c m u"))
-        for t in range(T_TILES):
+            nc.scalar.copy(out=grouped_words, in_=x_t_ps[:].rearrange("p c u m -> p c m u"))
+
+        def quantise_x(t):
             nc.vector.quantize_mx(
                 out=x_codes[:, t].rearrange("p c m -> p (c m)").bitcast(FP8X4),
                 scales=x_scales[:, t].rearrange("p c m -> p (c m)"),
                 in_=x_grouped[:, t, :],
             )
 
-        def projection(side, h, t):
+        scaled = {}
+        total = {}
+        gate_act = {}
+
+        def adapters(unit):
+            h, t = divmod(unit, T_TILES)
+            for i, side in enumerate(sides):
+                lora = psum.tile([P, N_TILE], F32, tag="lora")
+                nc.tensor.matmul(out=lora[:], lhsT=xa_t[side][:, t, :], rhs=b_tile[side, h][:], start=True, stop=True)
+                col = i * T_TILES + t
+                scaled[side, unit] = work.tile([P, N_TILE], F32, name="scaled_" + side)
+                nc.scalar.activation(
+                    out=scaled[side, unit][:], in_=lora[:], func=ACT.Copy, scale=token_scale[:, col : col + 1]
+                )
+
+        def projection(side, unit):
+            h, t = divmod(unit, T_TILES)
             codes, scales = mx_w[side, h]
-            lora = psum.tile([P, N_TILE], F32, tag="lora")
-            nc.tensor.matmul(out=lora[:], lhsT=xa_t[side][:, t, :], rhs=b_tile[side, h][:], start=True, stop=True)
             acc = psum.tile([P, N_TILE], F32, tag="mx")
             for c in range(PASSES):
                 nc.tensor.matmul_mx(
@@ -169,27 +191,36 @@ def tile_feedforward_pa_kernel(
                     start=(c == 0),
                     stop=(c == PASSES - 1),
                 )
-            col = sides.index(side) * T_TILES + t
-            scaled = work.tile([P, N_TILE], F32, tag="scaled")
-            nc.scalar.activation(out=scaled[:], in_=lora[:], func=ACT.Copy, scale=token_scale[:, col : col + 1])
-            total = work.tile([P, N_TILE], F32, tag="total")
-            nc.vector.tensor_tensor(out=total[:], in0=acc[:], in1=scaled[:], op=ALU.add)
-            return total
+            total[side, unit] = work.tile([P, N_TILE], F32, name="total_" + side)
+            nc.vector.tensor_tensor(out=total[side, unit][:], in0=acc[:], in1=scaled[side, unit][:], op=ALU.add)
 
-        for h in range(H_TILES):
-            mx_w["up", h] = quantise_weight_tile(nc, grouped_pool, mx_pool, w_raw["up", h])
-            gate_act = []
-            for t in range(T_TILES):
-                total = projection("gate", h, t)
-                act = act_pool.tile([P, N_TILE], F32, tag="act")
-                nc.scalar.activation(out=act[:], in_=total[:], func=ACT.Silu)
-                gate_act.append(act)
-            if h + 1 < H_TILES:
-                mx_w["gate", h + 1] = quantise_weight_tile(nc, grouped_pool, mx_pool, w_raw["gate", h + 1])
-            for t in range(T_TILES):
-                total = projection("up", h, t)
-                hidden = work.tile([P, N_TILE], F32, tag="hidden")
-                nc.vector.tensor_tensor(out=hidden[:], in0=gate_act[t][:], in1=total[:], op=ALU.mult)
-                nc.sync.dma_start(
-                    out=out_rows[t * P : (t + 1) * P, h * N_TILE : (h + 1) * N_TILE], in_=hidden[:]
-                )
+        def silu(unit):
+            gate_act[unit] = work.tile([P, N_TILE], F32, name="gate_act")
+            nc.scalar.activation(out=gate_act[unit][:], in_=total["gate", unit][:], func=ACT.Silu)
+
+        def finish(unit):
+            h, t = divmod(unit, T_TILES)
+            hidden = out_pool.tile([P, N_TILE], F32)
+            nc.gpsimd.tensor_tensor(out=hidden[:], in0=gate_act[unit][:], in1=total["up", unit][:], op=ALU.mult)
+            nc.sync.dma_start(out=out_rows[t * P : (t + 1) * P, h * N_TILE : (h + 1) * N_TILE], in_=hidden[:])
+
+        for half_step in range(LEAD):
+            prepare(half_step)
+        adapters(0)
+        transpose_x(0)
+        quantise_x(0)
+        for unit in range(UNITS + 1):
+            if unit + 1 < T_TILES:
+                transpose_x(unit + 1)
+            if unit + 1 < UNITS:
+                adapters(unit + 1)
+            if unit < UNITS:
+                projection("gate", unit)
+                silu(unit)
+            prepare(unit + LEAD)
+            if unit < UNITS:
+                projection("up", unit)
+            if unit + 1 < T_TILES:
+                quantise_x(unit + 1)
+            if unit >= 1:
+                finish(unit - 1)

@@ -25,8 +25,6 @@ N_TILE = 512
 H_TILES = HID // N_TILE
 UNITS = H_TILES * T_TILES
 RUN = 4
-SCALAR_COLS = 320
-LEAD = 4
 
 FLOPS = 2 * TOKENS * HID * 2 * (DIM + RANK)
 
@@ -55,12 +53,11 @@ def tile_feedforward_pa_kernel(
         keep = ctx.enter_context(tc.tile_pool(name="keep", bufs=1))
         raw_pool = ctx.enter_context(tc.tile_pool(name="raw", bufs=2 * H_TILES))
         b_pool = ctx.enter_context(tc.tile_pool(name="adapter", bufs=2 * H_TILES))
-        grouped_pool = ctx.enter_context(tc.tile_pool(name="grouped", bufs=2))
+        grouped_pool = ctx.enter_context(tc.tile_pool(name="grouped", bufs=3))
         mx_pool = ctx.enter_context(tc.tile_pool(name="mx", bufs=4))
-        work = ctx.enter_context(tc.tile_pool(name="work", bufs=3))
+        work = ctx.enter_context(tc.tile_pool(name="work", bufs=4))
         out_pool = ctx.enter_context(tc.tile_pool(name="out", bufs=8))
         psum = ctx.enter_context(tc.psum_pool(name="psum", bufs=4))
-        ctx.enter_context(tc.manual_schedule())
 
         ident_bf16 = keep.tile([P, P], BF16)
         make_identity(nc, ident_bf16[:])
@@ -115,32 +112,21 @@ def tile_feedforward_pa_kernel(
             out=token_scale[:], in_=tw_ps[:, 0 : 2 * T_TILES], func=ACT.Copy, scale=SCALING
         )
 
-        grouped = {}
         mx_w = {}
 
-        def prepare(half_step):
-            i = half_step // 2
-            if i >= 2 * H_TILES:
-                return
-            key = (sides[i % 2], i // 2)
-            if half_step % 2 == 0:
-                raw = w_raw[key]
-                grouped[key] = grouped_pool.tile([P, PASSES, N_TILE, PACK], BF16, name="grouped", align_bytes=64)
-                split = N_TILE - SCALAR_COLS
-                nc.scalar.copy(out=regrouped(grouped[key][:, 1, split:, :]), in_=as_loaded(raw[:, 1, :, split:]))
-                nc.vector.tensor_copy(out=regrouped(grouped[key][:, 0]), in_=as_loaded(raw[:, 0]))
-                nc.vector.tensor_copy(
-                    out=regrouped(grouped[key][:, 1, :split, :]), in_=as_loaded(raw[:, 1, :, :split])
-                )
-            else:
-                codes = mx_pool.tile([P, PASSES, N_TILE], U32, align_bytes=64)
-                scales = mx_pool.tile([P, PASSES, N_TILE], U8, align_bytes=64)
-                nc.vector.quantize_mx(
-                    out=codes[:].rearrange("p c n -> p (c n)").bitcast(FP8X4),
-                    scales=scales[:].rearrange("p c n -> p (c n)"),
-                    in_=grouped[key][:].rearrange("p c n j -> p (c n j)"),
-                )
-                mx_w[key] = (codes, scales)
+        def prepare(side, h):
+            raw = w_raw[side, h]
+            grouped = grouped_pool.tile([P, PASSES, N_TILE, PACK], BF16, align_bytes=64)
+            nc.vector.tensor_copy(out=regrouped(grouped[:, 0]), in_=as_loaded(raw[:, 0]))
+            nc.scalar.copy(out=regrouped(grouped[:, 1]), in_=as_loaded(raw[:, 1]))
+            codes = mx_pool.tile([P, PASSES, N_TILE], U32, align_bytes=64)
+            scales = mx_pool.tile([P, PASSES, N_TILE], U8, align_bytes=64)
+            nc.vector.quantize_mx(
+                out=codes[:].rearrange("p c n -> p (c n)").bitcast(FP8X4),
+                scales=scales[:].rearrange("p c n -> p (c n)"),
+                in_=grouped[:].rearrange("p c n j -> p (c n j)"),
+            )
+            mx_w[side, h] = (codes, scales)
 
         x_grouped = keep.tile([P, T_TILES, PASSES * P * PACK], BF16, align_bytes=64)
         x_codes = keep.tile([P, T_TILES, PASSES, P], U32, align_bytes=64)
@@ -153,7 +139,10 @@ def tile_feedforward_pa_kernel(
                 for u in range(2):
                     nc.tensor.transpose(out=x_t_ps[:, c, u, :], in_=x_words[:, c, u, :], identity=ident_f32[:])
             grouped_words = x_grouped[:, t, :].bitcast(F32).rearrange("p (c m u) -> p c m u", c=PASSES, u=2)
-            nc.scalar.copy(out=grouped_words, in_=x_t_ps[:].rearrange("p c u m -> p c m u"))
+            if t % 2 == 0:
+                nc.scalar.copy(out=grouped_words, in_=x_t_ps[:].rearrange("p c u m -> p c m u"))
+            else:
+                nc.vector.tensor_copy(out=grouped_words, in_=x_t_ps[:].rearrange("p c u m -> p c m u"))
 
         def quantise_x(t):
             nc.vector.quantize_mx(
@@ -162,24 +151,10 @@ def tile_feedforward_pa_kernel(
                 in_=x_grouped[:, t, :],
             )
 
-        scaled = {}
-        total = {}
-        gate_act = {}
-
-        def adapters(unit):
-            h, t = divmod(unit, T_TILES)
-            for i, side in enumerate(sides):
-                lora = psum.tile([P, N_TILE], F32, tag="lora")
-                nc.tensor.matmul(out=lora[:], lhsT=xa_t[side][:, t, :], rhs=b_tile[side, h][:], start=True, stop=True)
-                col = i * T_TILES + t
-                scaled[side, unit] = work.tile([P, N_TILE], F32, name="scaled_" + side)
-                nc.scalar.activation(
-                    out=scaled[side, unit][:], in_=lora[:], func=ACT.Copy, scale=token_scale[:, col : col + 1]
-                )
-
-        def projection(side, unit):
-            h, t = divmod(unit, T_TILES)
+        def projection(side, h, t):
             codes, scales = mx_w[side, h]
+            lora = psum.tile([P, N_TILE], F32, tag="lora")
+            nc.tensor.matmul(out=lora[:], lhsT=xa_t[side][:, t, :], rhs=b_tile[side, h][:], start=True, stop=True)
             acc = psum.tile([P, N_TILE], F32, tag="mx")
             for c in range(PASSES):
                 nc.tensor.matmul_mx(
@@ -191,36 +166,29 @@ def tile_feedforward_pa_kernel(
                     start=(c == 0),
                     stop=(c == PASSES - 1),
                 )
-            total[side, unit] = work.tile([P, N_TILE], F32, name="total_" + side)
-            nc.vector.tensor_tensor(out=total[side, unit][:], in0=acc[:], in1=scaled[side, unit][:], op=ALU.add)
+            lora_sb = work.tile([P, N_TILE], F32, name="lora_sb_" + side)
+            nc.scalar.copy(out=lora_sb[:], in_=lora[:])
+            col = sides.index(side) * T_TILES + t
+            total = work.tile([P, N_TILE], F32, name="total_" + side)
+            nc.vector.scalar_tensor_tensor(
+                out=total[:], in0=lora_sb[:], scalar=token_scale[:, col : col + 1], in1=acc[:], op0=ALU.mult, op1=ALU.add
+            )
+            return total
 
-        def silu(unit):
-            gate_act[unit] = work.tile([P, N_TILE], F32, name="gate_act")
-            nc.scalar.activation(out=gate_act[unit][:], in_=total["gate", unit][:], func=ACT.Silu)
-
-        def finish(unit):
-            h, t = divmod(unit, T_TILES)
-            hidden = out_pool.tile([P, N_TILE], F32)
-            nc.gpsimd.tensor_tensor(out=hidden[:], in0=gate_act[unit][:], in1=total["up", unit][:], op=ALU.mult)
-            nc.sync.dma_start(out=out_rows[t * P : (t + 1) * P, h * N_TILE : (h + 1) * N_TILE], in_=hidden[:])
-
-        for half_step in range(LEAD):
-            prepare(half_step)
-        adapters(0)
-        transpose_x(0)
-        quantise_x(0)
-        for unit in range(UNITS + 1):
-            if unit + 1 < T_TILES:
-                transpose_x(unit + 1)
-            if unit + 1 < UNITS:
-                adapters(unit + 1)
-            if unit < UNITS:
-                projection("gate", unit)
-                silu(unit)
-            prepare(unit + LEAD)
-            if unit < UNITS:
-                projection("up", unit)
-            if unit + 1 < T_TILES:
-                quantise_x(unit + 1)
-            if unit >= 1:
-                finish(unit - 1)
+        for side in sides:
+            prepare(side, 0)
+        for t in range(T_TILES):
+            transpose_x(t)
+            quantise_x(t)
+        for h in range(H_TILES):
+            if h + 1 < H_TILES:
+                for side in sides:
+                    prepare(side, h + 1)
+            for t in range(T_TILES):
+                gate = projection("gate", h, t)
+                gate_act = work.tile([P, N_TILE], F32)
+                nc.scalar.activation(out=gate_act[:], in_=gate[:], func=ACT.Silu)
+                up = projection("up", h, t)
+                hidden = out_pool.tile([P, N_TILE], F32)
+                nc.vector.tensor_tensor(out=hidden[:], in0=gate_act[:], in1=up[:], op=ALU.mult)
+                nc.sync.dma_start(out=out_rows[t * P : (t + 1) * P, h * N_TILE : (h + 1) * N_TILE], in_=hidden[:])

@@ -24,6 +24,7 @@ PASSES = DIM // K_PASS
 N_TILE = 512
 H_TILES = HID // N_TILE
 UNITS = H_TILES * T_TILES
+V_COLS = 128
 RUN = 4
 
 FLOPS = 2 * TOKENS * HID * 2 * (DIM + RANK)
@@ -118,7 +119,8 @@ def tile_feedforward_pa_kernel(
             raw = w_raw[side, h]
             grouped = grouped_pool.tile([P, PASSES, N_TILE, PACK], BF16, align_bytes=64)
             nc.vector.tensor_copy(out=regrouped(grouped[:, 0]), in_=as_loaded(raw[:, 0]))
-            nc.scalar.copy(out=regrouped(grouped[:, 1]), in_=as_loaded(raw[:, 1]))
+            nc.vector.tensor_copy(out=regrouped(grouped[:, 1, 0:V_COLS]), in_=as_loaded(raw[:, 1, :, 0:V_COLS]))
+            nc.scalar.copy(out=regrouped(grouped[:, 1, V_COLS:N_TILE]), in_=as_loaded(raw[:, 1, :, V_COLS:N_TILE]))
             codes = mx_pool.tile([P, PASSES, N_TILE], U32, align_bytes=64)
             scales = mx_pool.tile([P, PASSES, N_TILE], U8, align_bytes=64)
             nc.vector.quantize_mx(
@@ -190,5 +192,5 @@ def tile_feedforward_pa_kernel(
                 nc.scalar.activation(out=gate_act[:], in_=gate[:], func=ACT.Silu)
                 up = projection("up", h, t)
                 hidden = out_pool.tile([P, N_TILE], F32)
-                nc.vector.tensor_tensor(out=hidden[:], in0=gate_act[:], in1=up[:], op=ALU.mult)
+                nc.gpsimd.tensor_tensor(out=hidden[:], in0=gate_act[:], in1=up[:], op=ALU.mult)
                 nc.sync.dma_start(out=out_rows[t * P : (t + 1) * P, h * N_TILE : (h + 1) * N_TILE], in_=hidden[:])

@@ -10,6 +10,7 @@ U8 = mybir.dt.uint8
 FP8X4 = mybir.dt.float8_e4m3fn_x4
 ACT = mybir.ActivationFunctionType
 ALU = mybir.AluOpType
+ENGINE = mybir.EngineType
 
 P = 128
 PACK = 4
@@ -23,9 +24,9 @@ T_TILES = TOKENS // P
 PASSES = DIM // K_PASS
 N_TILE = 512
 H_TILES = HID // N_TILE
-UNITS = H_TILES * T_TILES
-V_COLS = 128
 RUN = 4
+V_COLS = 128
+TAIL_ON_GPSIMD = 1
 
 FLOPS = 2 * TOKENS * HID * 2 * (DIM + RANK)
 
@@ -49,6 +50,7 @@ def tile_feedforward_pa_kernel(
     xa = {"gate": xa_gate, "up": xa_up}
     b = {"gate": b_gate, "up": b_up}
     tw = {"gate": tw_gate, "up": tw_up}
+    tiles = range(T_TILES)
 
     with ExitStack() as ctx:
         keep = ctx.enter_context(tc.tile_pool(name="keep", bufs=1))
@@ -56,77 +58,87 @@ def tile_feedforward_pa_kernel(
         b_pool = ctx.enter_context(tc.tile_pool(name="adapter", bufs=2 * H_TILES))
         grouped_pool = ctx.enter_context(tc.tile_pool(name="grouped", bufs=3))
         mx_pool = ctx.enter_context(tc.tile_pool(name="mx", bufs=4))
-        work = ctx.enter_context(tc.tile_pool(name="work", bufs=4))
+        lora_pool = ctx.enter_context(tc.tile_pool(name="lora_sb", bufs=2 * T_TILES))
+        gate_pool = ctx.enter_context(tc.tile_pool(name="gate", bufs=2 * T_TILES))
+        up_pool = ctx.enter_context(tc.tile_pool(name="up", bufs=T_TILES))
         out_pool = ctx.enter_context(tc.tile_pool(name="out", bufs=8))
         psum = ctx.enter_context(tc.psum_pool(name="psum", bufs=4))
 
+        tw_rows = keep.tile([P, P], BF16)
+        nc.gpsimd.memset(tw_rows[:], 0.0)
         ident_bf16 = keep.tile([P, P], BF16)
         make_identity(nc, ident_bf16[:])
         ident_f32 = keep.tile([P, P], F32)
         make_identity(nc, ident_f32[:])
-        tw_rows = keep.tile([P, P], BF16)
-        nc.gpsimd.memset(tw_rows[:], 0.0)
 
-        xa_raw = {}
-        for i, side in enumerate(sides):
-            xa_raw[side] = keep.tile([P, T_TILES, RANK], BF16, name="xa_raw_" + side)
-            nc.sync.dma_start(
-                out=xa_raw[side][:],
-                in_=xa[side].flatten_outer_dims().rearrange("(t p) r -> p t r", p=P),
-            )
-            nc.sync.dma_start(
-                out=tw_rows[i * T_TILES : (i + 1) * T_TILES, :],
-                in_=tw[side].rearrange("(t u) s -> t (u s)", t=T_TILES),
-            )
-        x_raw = keep.tile([P, T_TILES, DIM], BF16)
         w_raw = {}
         b_tile = {}
-        for h in range(H_TILES):
+        xa_raw = {}
+        x_raw = keep.tile([P, T_TILES, DIM], BF16)
+
+        def load_weight(side, h):
             columns = slice(h * N_TILE, (h + 1) * N_TILE)
-            for side in sides:
-                b_tile[side, h] = b_pool.tile([P, N_TILE], BF16, name="b_tile")
-                nc.sync.dma_start(out=b_tile[side, h][:], in_=b[side][:, columns])
-            for side in sides:
-                w_raw[side, h] = raw_pool.tile([P, PASSES, PACK, N_TILE], BF16, name="w_raw")
-                for c in range(PASSES):
-                    nc.sync.dma_start(
-                        out=w_raw[side, h][:, c],
-                        in_=weight[side][c * K_PASS : (c + 1) * K_PASS, columns].rearrange(
-                            "(p j) n -> p j n", j=PACK
-                        ),
-                    )
-            if h == 0:
-                for t in range(T_TILES):
-                    nc.sync.dma_start(out=x_raw[:, t, :], in_=x_rows[t * P : (t + 1) * P, :])
+            w_raw[side, h] = raw_pool.tile([P, PASSES, PACK, N_TILE], BF16, name="w_raw")
+            for c in range(PASSES):
+                nc.sync.dma_start(
+                    out=w_raw[side, h][:, c],
+                    in_=weight[side][c * K_PASS : (c + 1) * K_PASS, columns].rearrange("(p j) n -> p j n", j=PACK),
+                )
 
-        xa_t = {}
-        for side in sides:
-            xa_t_ps = psum.tile([P, T_TILES, P], BF16, tag="lora")
-            for t in range(T_TILES):
-                nc.tensor.transpose(out=xa_t_ps[:, t, :], in_=xa_raw[side][:, t, :], identity=ident_bf16[:])
-            xa_t[side] = keep.tile([P, T_TILES, P], BF16, name="xa_t_" + side)
-            nc.scalar.copy(out=xa_t[side][:], in_=xa_t_ps[:])
-        tw_ps = psum.tile([P, P], BF16, tag="lora")
-        nc.tensor.transpose(out=tw_ps[:], in_=tw_rows[:], identity=ident_bf16[:])
-        token_scale = keep.tile([P, 2 * T_TILES], F32)
-        nc.scalar.activation(
-            out=token_scale[:], in_=tw_ps[:, 0 : 2 * T_TILES], func=ACT.Copy, scale=SCALING
-        )
+        def load_b(side, h):
+            b_tile[side, h] = b_pool.tile([P, N_TILE], BF16, name="b_tile")
+            nc.sync.dma_start(out=b_tile[side, h][:], in_=b[side][:, h * N_TILE : (h + 1) * N_TILE])
 
+        def load_xa(side):
+            xa_raw[side] = keep.tile([P, T_TILES, RANK], BF16, name="xa_raw_" + side)
+            nc.sync.dma_start(
+                out=xa_raw[side][:], in_=xa[side].flatten_outer_dims().rearrange("(t p) r -> p t r", p=P)
+            )
+
+        def load_tw(side):
+            i = sides.index(side)
+            nc.sync.dma_start(
+                out=tw_rows[i * T_TILES : (i + 1) * T_TILES, :], in_=tw[side].rearrange("(t u) s -> t (u s)", t=T_TILES)
+            )
+
+        with tc.manual_schedule(engines={ENGINE.SP}):
+            load_weight("gate", 0)
+            for side in sides:
+                load_tw(side)
+            load_weight("up", 0)
+            for t in tiles:
+                nc.sync.dma_start(out=x_raw[:, t, :], in_=x_rows[t * P : (t + 1) * P, :])
+            for side in sides:
+                load_xa(side)
+                load_b(side, 0)
+            for h in range(1, H_TILES):
+                for side in sides:
+                    load_b(side, h)
+                for side in sides:
+                    load_weight(side, h)
+
+        grouped = {}
         mx_w = {}
 
-        def prepare(side, h):
-            raw = w_raw[side, h]
-            grouped = grouped_pool.tile([P, PASSES, N_TILE, PACK], BF16, align_bytes=64)
-            nc.vector.tensor_copy(out=regrouped(grouped[:, 0]), in_=as_loaded(raw[:, 0]))
-            nc.vector.tensor_copy(out=regrouped(grouped[:, 1, 0:V_COLS]), in_=as_loaded(raw[:, 1, :, 0:V_COLS]))
-            nc.scalar.copy(out=regrouped(grouped[:, 1, V_COLS:N_TILE]), in_=as_loaded(raw[:, 1, :, V_COLS:N_TILE]))
-            codes = mx_pool.tile([P, PASSES, N_TILE], U32, align_bytes=64)
-            scales = mx_pool.tile([P, PASSES, N_TILE], U8, align_bytes=64)
+        def scalar_share(side, h):
+            grouped[side, h] = grouped_pool.tile([P, PASSES, N_TILE, PACK], BF16, align_bytes=64, name="grouped")
+            nc.scalar.copy(
+                out=regrouped(grouped[side, h][:, 0, V_COLS:N_TILE]), in_=as_loaded(w_raw[side, h][:, 0, :, V_COLS:N_TILE])
+            )
+
+        def vector_share(side, h):
+            nc.vector.tensor_copy(
+                out=regrouped(grouped[side, h][:, 0, 0:V_COLS]), in_=as_loaded(w_raw[side, h][:, 0, :, 0:V_COLS])
+            )
+            nc.vector.tensor_copy(out=regrouped(grouped[side, h][:, 1]), in_=as_loaded(w_raw[side, h][:, 1]))
+
+        def quantise(side, h):
+            codes = mx_pool.tile([P, PASSES, N_TILE], U32, align_bytes=64, name="codes")
+            scales = mx_pool.tile([P, PASSES, N_TILE], U8, align_bytes=64, name="scales")
             nc.vector.quantize_mx(
                 out=codes[:].rearrange("p c n -> p (c n)").bitcast(FP8X4),
                 scales=scales[:].rearrange("p c n -> p (c n)"),
-                in_=grouped[:].rearrange("p c n j -> p (c n j)"),
+                in_=grouped[side, h][:].rearrange("p c n j -> p (c n j)"),
             )
             mx_w[side, h] = (codes, scales)
 
@@ -153,14 +165,42 @@ def tile_feedforward_pa_kernel(
                 in_=x_grouped[:, t, :],
             )
 
+        xa_t = {}
+        token_scale = keep.tile([P, 2 * T_TILES], F32)
+
+        def transpose_xa(side):
+            xa_t_ps = psum.tile([P, T_TILES, P], BF16, tag="lora")
+            for t in tiles:
+                nc.tensor.transpose(out=xa_t_ps[:, t, :], in_=xa_raw[side][:, t, :], identity=ident_bf16[:])
+            xa_t[side] = keep.tile([P, T_TILES, P], BF16, name="xa_t_" + side)
+            nc.scalar.copy(out=xa_t[side][:], in_=xa_t_ps[:])
+
+        def transpose_tw():
+            tw_ps = psum.tile([P, P], BF16, tag="lora")
+            nc.tensor.transpose(out=tw_ps[:], in_=tw_rows[:], identity=ident_bf16[:])
+            nc.scalar.activation(out=token_scale[:], in_=tw_ps[:, 0 : 2 * T_TILES], func=ACT.Copy, scale=SCALING)
+
+        lora_ps = {}
+        lora_sb = {}
+        acc = {}
+        total = {}
+
+        def adapter_matmul(side, h, t):
+            lora_ps[side, h, t] = psum.tile([P, N_TILE], F32, tag="lora", name="lora_ps")
+            nc.tensor.matmul(
+                out=lora_ps[side, h, t][:], lhsT=xa_t[side][:, t, :], rhs=b_tile[side, h][:], start=True, stop=True
+            )
+
+        def adapter_out(side, h, t):
+            lora_sb[side, h, t] = lora_pool.tile([P, N_TILE], F32, name="lora_sb")
+            nc.scalar.copy(out=lora_sb[side, h, t][:], in_=lora_ps[side, h, t][:])
+
         def projection(side, h, t):
             codes, scales = mx_w[side, h]
-            lora = psum.tile([P, N_TILE], F32, tag="lora")
-            nc.tensor.matmul(out=lora[:], lhsT=xa_t[side][:, t, :], rhs=b_tile[side, h][:], start=True, stop=True)
-            acc = psum.tile([P, N_TILE], F32, tag="mx")
+            acc[side, h, t] = psum.tile([P, N_TILE], F32, tag="mx", name="acc")
             for c in range(PASSES):
                 nc.tensor.matmul_mx(
-                    out=acc[:],
+                    out=acc[side, h, t][:],
                     lhsT=x_codes[:, t, c, :].bitcast(FP8X4),
                     lhsT_scale=x_scales[:, t, c, :],
                     rhs=codes[:, c, :].bitcast(FP8X4),
@@ -168,29 +208,84 @@ def tile_feedforward_pa_kernel(
                     start=(c == 0),
                     stop=(c == PASSES - 1),
                 )
-            lora_sb = work.tile([P, N_TILE], F32, name="lora_sb_" + side)
-            nc.scalar.copy(out=lora_sb[:], in_=lora[:])
-            col = sides.index(side) * T_TILES + t
-            total = work.tile([P, N_TILE], F32, name="total_" + side)
-            nc.vector.scalar_tensor_tensor(
-                out=total[:], in0=lora_sb[:], scalar=token_scale[:, col : col + 1], in1=acc[:], op0=ALU.mult, op1=ALU.add
-            )
-            return total
 
-        for side in sides:
-            prepare(side, 0)
-        for t in range(T_TILES):
-            transpose_x(t)
-            quantise_x(t)
-        for h in range(H_TILES):
-            if h + 1 < H_TILES:
-                for side in sides:
-                    prepare(side, h + 1)
-            for t in range(T_TILES):
-                gate = projection("gate", h, t)
-                gate_act = work.tile([P, N_TILE], F32)
-                nc.scalar.activation(out=gate_act[:], in_=gate[:], func=ACT.Silu)
-                up = projection("up", h, t)
-                hidden = out_pool.tile([P, N_TILE], F32)
-                nc.gpsimd.tensor_tensor(out=hidden[:], in0=gate_act[:], in1=up[:], op=ALU.mult)
-                nc.sync.dma_start(out=out_rows[t * P : (t + 1) * P, h * N_TILE : (h + 1) * N_TILE], in_=hidden[:])
+        def add_up(side, h, t):
+            pool = gate_pool if side == "gate" else up_pool
+            total[side, h, t] = pool.tile([P, N_TILE], F32, name="total_" + side)
+            col = sides.index(side) * T_TILES + t
+            nc.vector.scalar_tensor_tensor(
+                out=total[side, h, t][:],
+                in0=lora_sb[side, h, t][:],
+                scalar=token_scale[:, col : col + 1],
+                in1=acc[side, h, t][:],
+                op0=ALU.mult,
+                op1=ALU.add,
+            )
+
+        def silu(h, t):
+            nc.scalar.activation(out=total["gate", h, t][:], in_=total["gate", h, t][:], func=ACT.Silu)
+
+        def product(engine, h, t):
+            hidden = out_pool.tile([P, N_TILE], F32, name="hidden")
+            engine.tensor_tensor(out=hidden[:], in0=total["gate", h, t][:], in1=total["up", h, t][:], op=ALU.mult)
+            nc.sync.dma_start(out=out_rows[t * P : (t + 1) * P, h * N_TILE : (h + 1) * N_TILE], in_=hidden[:])
+
+        with tc.manual_schedule(engines={ENGINE.DVE, ENGINE.Pool, ENGINE.Activation, ENGINE.PE}):
+            for side in sides:
+                scalar_share(side, 0)
+                vector_share(side, 0)
+            transpose_tw()
+            for side in sides:
+                quantise(side, 0)
+            for t in tiles:
+                transpose_x(t)
+            for t in tiles:
+                quantise_x(t)
+            transpose_xa("gate")
+            for t in tiles:
+                adapter_matmul("gate", 0, t)
+            for t in tiles:
+                adapter_out("gate", 0, t)
+            transpose_xa("up")
+
+            for h in range(H_TILES + 1):
+                if h > 0:
+                    for t in range(T_TILES // 2, T_TILES):
+                        silu(h - 1, t)
+                if 0 < h < H_TILES:
+                    for t in tiles:
+                        adapter_out("up", h - 1, t)
+                if 0 < h < H_TILES:
+                    for t in tiles:
+                        adapter_matmul("gate", h, t)
+                    for t in tiles:
+                        adapter_out("gate", h, t)
+                    for side in sides:
+                        vector_share(side, h)
+                    for side in sides:
+                        quantise(side, h)
+                if h > 0:
+                    for t in tiles:
+                        add_up("up", h - 1, t)
+                        if h < H_TILES or t < TAIL_ON_GPSIMD:
+                            product(nc.gpsimd, h - 1, t)
+                    if h == H_TILES:
+                        for t in range(TAIL_ON_GPSIMD, T_TILES):
+                            product(nc.vector, h - 1, t)
+                if h < H_TILES:
+                    for t in tiles:
+                        projection("gate", h, t)
+                    for t in tiles:
+                        add_up("gate", h, t)
+                    for t in tiles:
+                        adapter_matmul("up", h, t)
+                    for t in tiles:
+                        projection("up", h, t)
+                    if h + 1 < H_TILES:
+                        for side in sides:
+                            scalar_share(side, h + 1)
+                    else:
+                        for t in tiles:
+                            adapter_out("up", h, t)
+                    for t in range(T_TILES // 2):
+                        silu(h, t)

@@ -24,7 +24,7 @@ T_TILES = TOKENS // P
 PASSES = DIM // K_PASS
 N_TILE = 512
 H_TILES = HID // N_TILE
-RUN = 4
+RUN = 8
 V_COLS = 128
 TAIL_ON_GPSIMD = 1
 

@@ -25,7 +25,7 @@ PASSES = DIM // K_PASS
 N_TILE = 512
 H_TILES = HID // N_TILE
 RUN = 8
-V_COLS = 128
+V_COLS = 96
 TAIL_ON_GPSIMD = 1
 
 FLOPS = 2 * TOKENS * HID * 2 * (DIM + RANK)
@@ -59,7 +59,7 @@ def tile_feedforward_pa_kernel(
         grouped_pool = ctx.enter_context(tc.tile_pool(name="grouped", bufs=3))
         mx_pool = ctx.enter_context(tc.tile_pool(name="mx", bufs=4))
         lora_pool = ctx.enter_context(tc.tile_pool(name="lora_sb", bufs=2 * T_TILES))
-        gate_pool = ctx.enter_context(tc.tile_pool(name="gate", bufs=2 * T_TILES))
+        gate_pool = ctx.enter_context(tc.tile_pool(name="gate", bufs=2))
         up_pool = ctx.enter_context(tc.tile_pool(name="up", bufs=T_TILES))
         out_pool = ctx.enter_context(tc.tile_pool(name="out", bufs=8))
         psum = ctx.enter_context(tc.psum_pool(name="psum", bufs=4))
@@ -102,15 +102,16 @@ def tile_feedforward_pa_kernel(
             )
 
         with tc.manual_schedule(engines={ENGINE.SP}):
-            load_weight("gate", 0)
-            for side in sides:
-                load_tw(side)
-            load_weight("up", 0)
             for t in tiles:
                 nc.sync.dma_start(out=x_raw[:, t, :], in_=x_rows[t * P : (t + 1) * P, :])
             for side in sides:
-                load_xa(side)
-                load_b(side, 0)
+                load_tw(side)
+            load_xa("gate")
+            load_b("gate", 0)
+            load_weight("gate", 0)
+            load_weight("up", 0)
+            load_xa("up")
+            load_b("up", 0)
             for h in range(1, H_TILES):
                 for side in sides:
                     load_b(side, h)
@@ -184,6 +185,7 @@ def tile_feedforward_pa_kernel(
         lora_sb = {}
         acc = {}
         total = {}
+        gate_range = {}
 
         def adapter_matmul(side, h, t):
             lora_ps[side, h, t] = psum.tile([P, N_TILE], F32, tag="lora", name="lora_ps")
@@ -210,11 +212,16 @@ def tile_feedforward_pa_kernel(
                 )
 
         def add_up(side, h, t):
-            pool = gate_pool if side == "gate" else up_pool
-            total[side, h, t] = pool.tile([P, N_TILE], F32, name="total_" + side)
+            if side == "up":
+                up_total = up_pool.tile([P, N_TILE], F32, name="total_up")
+                total[side, h, t] = up_total[:]
+            else:
+                if t == 0:
+                    gate_range[h] = gate_pool.tile([P, T_TILES, N_TILE], F32, name="total_gate")
+                total[side, h, t] = gate_range[h][:, t, :]
             col = sides.index(side) * T_TILES + t
             nc.vector.scalar_tensor_tensor(
-                out=total[side, h, t][:],
+                out=total[side, h, t],
                 in0=lora_sb[side, h, t][:],
                 scalar=token_scale[:, col : col + 1],
                 in1=acc[side, h, t][:],
@@ -222,36 +229,39 @@ def tile_feedforward_pa_kernel(
                 op1=ALU.add,
             )
 
-        def silu(h, t):
-            nc.scalar.activation(out=total["gate", h, t][:], in_=total["gate", h, t][:], func=ACT.Silu)
+        def silu(h, first, count):
+            part = gate_range[h][:, first : first + count, :]
+            nc.scalar.activation(out=part, in_=part, func=ACT.Silu)
 
         def product(engine, h, t):
             hidden = out_pool.tile([P, N_TILE], F32, name="hidden")
-            engine.tensor_tensor(out=hidden[:], in0=total["gate", h, t][:], in1=total["up", h, t][:], op=ALU.mult)
+            engine.tensor_tensor(out=hidden[:], in0=total["gate", h, t], in1=total["up", h, t], op=ALU.mult)
             nc.sync.dma_start(out=out_rows[t * P : (t + 1) * P, h * N_TILE : (h + 1) * N_TILE], in_=hidden[:])
 
         with tc.manual_schedule(engines={ENGINE.DVE, ENGINE.Pool, ENGINE.Activation, ENGINE.PE}):
-            for side in sides:
-                scalar_share(side, 0)
-                vector_share(side, 0)
-            transpose_tw()
-            for side in sides:
-                quantise(side, 0)
             for t in tiles:
                 transpose_x(t)
             for t in tiles:
                 quantise_x(t)
+            transpose_tw()
             transpose_xa("gate")
+            scalar_share("gate", 0)
+            vector_share("gate", 0)
+            quantise("gate", 0)
             for t in tiles:
                 adapter_matmul("gate", 0, t)
             for t in tiles:
                 adapter_out("gate", 0, t)
+            scalar_share("up", 0)
+            vector_share("up", 0)
             transpose_xa("up")
 
             for h in range(H_TILES + 1):
-                if h > 0:
+                if 0 < h < H_TILES:
+                    silu(h - 1, 0, T_TILES)
+                if h == H_TILES:
                     for t in range(T_TILES // 2, T_TILES):
-                        silu(h - 1, t)
+                        silu(h - 1, t, 1)
                 if 0 < h < H_TILES:
                     for t in tiles:
                         adapter_out("up", h - 1, t)
@@ -277,6 +287,8 @@ def tile_feedforward_pa_kernel(
                         projection("gate", h, t)
                     for t in tiles:
                         add_up("gate", h, t)
+                    if h == 0:
+                        quantise("up", 0)
                     for t in tiles:
                         adapter_matmul("up", h, t)
                     for t in tiles:
@@ -287,5 +299,6 @@ def tile_feedforward_pa_kernel(
                     else:
                         for t in tiles:
                             adapter_out("up", h, t)
-                    for t in range(T_TILES // 2):
-                        silu(h, t)
+                    if h + 1 == H_TILES:
+                        for t in range(T_TILES // 2):
+                            silu(h, t, 1)

@@ -285,12 +285,15 @@ def tile_feedforward_pa_kernel(
                 if h < H_TILES:
                     for t in tiles:
                         projection("gate", h, t)
+                        if h + 1 == H_TILES:
+                            adapter_matmul("up", h, t)
                     for t in tiles:
                         add_up("gate", h, t)
                     if h == 0:
                         quantise("up", 0)
-                    for t in tiles:
-                        adapter_matmul("up", h, t)
+                    if h + 1 < H_TILES:
+                        for t in tiles:
+                            adapter_matmul("up", h, t)
                     for t in tiles:
                         projection("up", h, t)
                     if h + 1 < H_TILES:

@@ -25,7 +25,7 @@ PASSES = DIM // K_PASS
 N_TILE = 512
 H_TILES = HID // N_TILE
 RUN = 8
-V_COLS = 96
+S_COLS = 416
 TAIL_ON_GPSIMD = 1
 
 FLOPS = 2 * TOKENS * HID * 2 * (DIM + RANK)
@@ -78,10 +78,10 @@ def tile_feedforward_pa_kernel(
 
         def load_weight(side, h):
             columns = slice(h * N_TILE, (h + 1) * N_TILE)
-            w_raw[side, h] = raw_pool.tile([P, PASSES, PACK, N_TILE], BF16, name="w_raw")
+            w_raw[side, h] = raw_pool.tile([P, PACK, PASSES, N_TILE], BF16, name="w_raw")
             for c in range(PASSES):
                 nc.sync.dma_start(
-                    out=w_raw[side, h][:, c],
+                    out=w_raw[side, h][:, :, c, :],
                     in_=weight[side][c * K_PASS : (c + 1) * K_PASS, columns].rearrange("(p j) n -> p j n", j=PACK),
                 )
 
@@ -122,16 +122,17 @@ def tile_feedforward_pa_kernel(
         mx_w = {}
 
         def scalar_share(side, h):
-            grouped[side, h] = grouped_pool.tile([P, PASSES, N_TILE, PACK], BF16, align_bytes=64, name="grouped")
+            grouped[side, h] = grouped_pool.tile([P, PASSES * N_TILE, PACK], BF16, align_bytes=64, name="grouped")
             nc.scalar.copy(
-                out=regrouped(grouped[side, h][:, 0, V_COLS:N_TILE]), in_=as_loaded(w_raw[side, h][:, 0, :, V_COLS:N_TILE])
+                out=regrouped(grouped[side, h][:, 0:S_COLS]),
+                in_=as_loaded(w_raw[side, h][:].rearrange("p j c n -> p j (c n)")[:, :, 0:S_COLS]),
             )
 
         def vector_share(side, h):
             nc.vector.tensor_copy(
-                out=regrouped(grouped[side, h][:, 0, 0:V_COLS]), in_=as_loaded(w_raw[side, h][:, 0, :, 0:V_COLS])
+                out=regrouped(grouped[side, h][:, S_COLS : PASSES * N_TILE]),
+                in_=as_loaded(w_raw[side, h][:].rearrange("p j c n -> p j (c n)")[:, :, S_COLS : PASSES * N_TILE]),
             )
-            nc.vector.tensor_copy(out=regrouped(grouped[side, h][:, 1]), in_=as_loaded(w_raw[side, h][:, 1]))
 
         def quantise(side, h):
             codes = mx_pool.tile([P, PASSES, N_TILE], U32, align_bytes=64, name="codes")
@@ -139,7 +140,7 @@ def tile_feedforward_pa_kernel(
             nc.vector.quantize_mx(
                 out=codes[:].rearrange("p c n -> p (c n)").bitcast(FP8X4),
                 scales=scales[:].rearrange("p c n -> p (c n)"),
-                in_=grouped[side, h][:].rearrange("p c n j -> p (c n j)"),
+                in_=grouped[side, h][:].rearrange("p n j -> p (n j)"),
             )
             mx_w[side, h] = (codes, scales)
 

from contextlib import ExitStack

import concourse.mybir as mybir
from concourse.masks import make_identity

F32 = mybir.dt.float32
BF16 = mybir.dt.bfloat16
U32 = mybir.dt.uint32
U8 = mybir.dt.uint8
FP8X4 = mybir.dt.float8_e4m3fn_x4
ACT = mybir.ActivationFunctionType
ALU = mybir.AluOpType
ENGINE = mybir.EngineType

P = 128
PACK = 4
K_PASS = P * PACK
TOKENS = 512
DIM = 1024
HID = 2560
RANK = 128
SCALING = 4.0
T_TILES = TOKENS // P
PASSES = DIM // K_PASS
N_TILE = 512
H_TILES = HID // N_TILE
RUN = 8
S_COLS = 416
TAIL_ON_GPSIMD = 1

FLOPS = 2 * TOKENS * HID * 2 * (DIM + RANK)


def regrouped(ap):
    return ap.rearrange("p (g i) j -> p g j i", i=RUN)


def as_loaded(ap):
    return ap.rearrange("p j (g i) -> p g j i", i=RUN)


def tile_feedforward_pa_kernel(
    tc, x, w1, w3, xa_up, b_up, xa_gate, b_gate, tw_up, tw_gate, out
):
    nc = tc.nc
    x_rows = x.flatten_outer_dims()
    out_rows = out.flatten_outer_dims()
    sides = ("gate", "up")
    weight = {"gate": w1, "up": w3}
    xa = {"gate": xa_gate, "up": xa_up}
    b = {"gate": b_gate, "up": b_up}
    tw = {"gate": tw_gate, "up": tw_up}
    tiles = range(T_TILES)

    with ExitStack() as ctx:
        keep = ctx.enter_context(tc.tile_pool(name="keep", bufs=1))
        raw_pool = ctx.enter_context(tc.tile_pool(name="raw", bufs=2 * H_TILES))
        b_pool = ctx.enter_context(tc.tile_pool(name="adapter", bufs=2 * H_TILES))
        grouped_pool = ctx.enter_context(tc.tile_pool(name="grouped", bufs=3))
        mx_pool = ctx.enter_context(tc.tile_pool(name="mx", bufs=4))
        lora_pool = ctx.enter_context(tc.tile_pool(name="lora_sb", bufs=2 * T_TILES))
        gate_pool = ctx.enter_context(tc.tile_pool(name="gate", bufs=2))
        up_pool = ctx.enter_context(tc.tile_pool(name="up", bufs=T_TILES))
        out_pool = ctx.enter_context(tc.tile_pool(name="out", bufs=8))
        psum = ctx.enter_context(tc.psum_pool(name="psum", bufs=4))

        tw_rows = keep.tile([P, P], BF16)
        nc.gpsimd.memset(tw_rows[:], 0.0)
        ident_bf16 = keep.tile([P, P], BF16)
        make_identity(nc, ident_bf16[:])
        ident_f32 = keep.tile([P, P], F32)
        make_identity(nc, ident_f32[:])

        w_raw = {}
        b_tile = {}
        xa_raw = {}
        x_raw = keep.tile([P, T_TILES, DIM], BF16)

        def load_weight(side, h):
            columns = slice(h * N_TILE, (h + 1) * N_TILE)
            w_raw[side, h] = raw_pool.tile([P, PACK, PASSES, N_TILE], BF16, name="w_raw")
            for c in range(PASSES):
                nc.sync.dma_start(
                    out=w_raw[side, h][:, :, c, :],
                    in_=weight[side][c * K_PASS : (c + 1) * K_PASS, columns].rearrange("(p j) n -> p j n", j=PACK),
                )

        def load_b(side, h):
            b_tile[side, h] = b_pool.tile([P, N_TILE], BF16, name="b_tile")
            nc.sync.dma_start(out=b_tile[side, h][:], in_=b[side][:, h * N_TILE : (h + 1) * N_TILE])

        def load_xa(side):
            xa_raw[side] = keep.tile([P, T_TILES, RANK], BF16, name="xa_raw_" + side)
            nc.sync.dma_start(
                out=xa_raw[side][:], in_=xa[side].flatten_outer_dims().rearrange("(t p) r -> p t r", p=P)
            )

        def load_tw(side):
            i = sides.index(side)
            nc.sync.dma_start(
                out=tw_rows[i * T_TILES : (i + 1) * T_TILES, :], in_=tw[side].rearrange("(t u) s -> t (u s)", t=T_TILES)
            )

        with tc.manual_schedule(engines={ENGINE.SP}):
            for t in tiles:
                nc.sync.dma_start(out=x_raw[:, t, :], in_=x_rows[t * P : (t + 1) * P, :])
            for side in sides:
                load_tw(side)
            load_xa("gate")
            load_b("gate", 0)
            load_weight("gate", 0)
            load_weight("up", 0)
            load_xa("up")
            load_b("up", 0)
            for h in range(1, H_TILES):
                for side in sides:
                    load_b(side, h)
                for side in sides:
                    load_weight(side, h)

        grouped = {}
        mx_w = {}

        def scalar_share(side, h):
            grouped[side, h] = grouped_pool.tile([P, PASSES * N_TILE, PACK], BF16, align_bytes=64, name="grouped")
            nc.scalar.copy(
                out=regrouped(grouped[side, h][:, 0:S_COLS]),
                in_=as_loaded(w_raw[side, h][:].rearrange("p j c n -> p j (c n)")[:, :, 0:S_COLS]),
            )

        def vector_share(side, h):
            nc.vector.tensor_copy(
                out=regrouped(grouped[side, h][:, S_COLS : PASSES * N_TILE]),
                in_=as_loaded(w_raw[side, h][:].rearrange("p j c n -> p j (c n)")[:, :, S_COLS : PASSES * N_TILE]),
            )

        def quantise(side, h):
            codes = mx_pool.tile([P, PASSES, N_TILE], U32, align_bytes=64, name="codes")
            scales = mx_pool.tile([P, PASSES, N_TILE], U8, align_bytes=64, name="scales")
            nc.vector.quantize_mx(
                out=codes[:].rearrange("p c n -> p (c n)").bitcast(FP8X4),
                scales=scales[:].rearrange("p c n -> p (c n)"),
                in_=grouped[side, h][:].rearrange("p n j -> p (n j)"),
            )
            mx_w[side, h] = (codes, scales)

        x_grouped = keep.tile([P, T_TILES, PASSES * P * PACK], BF16, align_bytes=64)
        x_codes = keep.tile([P, T_TILES, PASSES, P], U32, align_bytes=64)
        x_scales = keep.tile([P, T_TILES, PASSES, P], U8, align_bytes=64)

        def transpose_x(t):
            x_words = x_raw[:, t, :].bitcast(F32).rearrange("p (c q u) -> p c u q", c=PASSES, u=2)
            x_t_ps = psum.tile([P, PASSES, 2, P], F32, tag="mx")
            for c in range(PASSES):
                for u in range(2):
                    nc.tensor.transpose(out=x_t_ps[:, c, u, :], in_=x_words[:, c, u, :], identity=ident_f32[:])
            grouped_words = x_grouped[:, t, :].bitcast(F32).rearrange("p (c m u) -> p c m u", c=PASSES, u=2)
            if t % 2 == 0:
                nc.scalar.copy(out=grouped_words, in_=x_t_ps[:].rearrange("p c u m -> p c m u"))
            else:
                nc.vector.tensor_copy(out=grouped_words, in_=x_t_ps[:].rearrange("p c u m -> p c m u"))

        def quantise_x(t):
            nc.vector.quantize_mx(
                out=x_codes[:, t].rearrange("p c m -> p (c m)").bitcast(FP8X4),
                scales=x_scales[:, t].rearrange("p c m -> p (c m)"),
                in_=x_grouped[:, t, :],
            )

        xa_t = {}
        token_scale = keep.tile([P, 2 * T_TILES], F32)

        def transpose_xa(side):
            xa_t_ps = psum.tile([P, T_TILES, P], BF16, tag="lora")
            for t in tiles:
                nc.tensor.transpose(out=xa_t_ps[:, t, :], in_=xa_raw[side][:, t, :], identity=ident_bf16[:])
            xa_t[side] = keep.tile([P, T_TILES, P], BF16, name="xa_t_" + side)
            nc.scalar.copy(out=xa_t[side][:], in_=xa_t_ps[:])

        def transpose_tw():
            tw_ps = psum.tile([P, P], BF16, tag="lora")
            nc.tensor.transpose(out=tw_ps[:], in_=tw_rows[:], identity=ident_bf16[:])
            nc.scalar.activation(out=token_scale[:], in_=tw_ps[:, 0 : 2 * T_TILES], func=ACT.Copy, scale=SCALING)

        lora_ps = {}
        lora_sb = {}
        acc = {}
        total = {}
        gate_range = {}

        def adapter_matmul(side, h, t):
            lora_ps[side, h, t] = psum.tile([P, N_TILE], F32, tag="lora", name="lora_ps")
            nc.tensor.matmul(
                out=lora_ps[side, h, t][:], lhsT=xa_t[side][:, t, :], rhs=b_tile[side, h][:], start=True, stop=True
            )

        def adapter_out(side, h, t):
            lora_sb[side, h, t] = lora_pool.tile([P, N_TILE], F32, name="lora_sb")
            nc.scalar.copy(out=lora_sb[side, h, t][:], in_=lora_ps[side, h, t][:])

        def projection(side, h, t):
            codes, scales = mx_w[side, h]
            acc[side, h, t] = psum.tile([P, N_TILE], F32, tag="mx", name="acc")
            for c in range(PASSES):
                nc.tensor.matmul_mx(
                    out=acc[side, h, t][:],
                    lhsT=x_codes[:, t, c, :].bitcast(FP8X4),
                    lhsT_scale=x_scales[:, t, c, :],
                    rhs=codes[:, c, :].bitcast(FP8X4),
                    rhs_scale=scales[:, c, :],
                    start=(c == 0),
                    stop=(c == PASSES - 1),
                )

        def add_up(side, h, t):
            if side == "up":
                up_total = up_pool.tile([P, N_TILE], F32, name="total_up")
                total[side, h, t] = up_total[:]
            else:
                if t == 0:
                    gate_range[h] = gate_pool.tile([P, T_TILES, N_TILE], F32, name="total_gate")
                total[side, h, t] = gate_range[h][:, t, :]
            col = sides.index(side) * T_TILES + t
            nc.vector.scalar_tensor_tensor(
                out=total[side, h, t],
                in0=lora_sb[side, h, t][:],
                scalar=token_scale[:, col : col + 1],
                in1=acc[side, h, t][:],
                op0=ALU.mult,
                op1=ALU.add,
            )

        def silu(h, first, count):
            part = gate_range[h][:, first : first + count, :]
            nc.scalar.activation(out=part, in_=part, func=ACT.Silu)

        def product(engine, h, t):
            hidden = out_pool.tile([P, N_TILE], F32, name="hidden")
            engine.tensor_tensor(out=hidden[:], in0=total["gate", h, t], in1=total["up", h, t], op=ALU.mult)
            nc.sync.dma_start(out=out_rows[t * P : (t + 1) * P, h * N_TILE : (h + 1) * N_TILE], in_=hidden[:])

        with tc.manual_schedule(engines={ENGINE.DVE, ENGINE.Pool, ENGINE.Activation, ENGINE.PE}):
            for t in tiles:
                transpose_x(t)
            for t in tiles:
                quantise_x(t)
            transpose_tw()
            transpose_xa("gate")
            scalar_share("gate", 0)
            vector_share("gate", 0)
            quantise("gate", 0)
            for t in tiles:
                adapter_matmul("gate", 0, t)
            for t in tiles:
                adapter_out("gate", 0, t)
            scalar_share("up", 0)
            vector_share("up", 0)
            transpose_xa("up")

            for h in range(H_TILES + 1):
                if 0 < h < H_TILES:
                    silu(h - 1, 0, T_TILES)
                if h == H_TILES:
                    for t in range(T_TILES // 2, T_TILES):
                        silu(h - 1, t, 1)
                if 0 < h < H_TILES:
                    for t in tiles:
                        adapter_out("up", h - 1, t)
                if 0 < h < H_TILES:
                    for t in tiles:
                        adapter_matmul("gate", h, t)
                    for t in tiles:
                        adapter_out("gate", h, t)
                    for side in sides:
                        vector_share(side, h)
                    for side in sides:
                        quantise(side, h)
                if h > 0:
                    for t in tiles:
                        add_up("up", h - 1, t)
                        if h < H_TILES or t < TAIL_ON_GPSIMD:
                            product(nc.gpsimd, h - 1, t)
                    if h == H_TILES:
                        for t in range(TAIL_ON_GPSIMD, T_TILES):
                            product(nc.vector, h - 1, t)
                if h < H_TILES:
                    for t in tiles:
                        projection("gate", h, t)
                        if h + 1 == H_TILES:
                            adapter_matmul("up", h, t)
                    for t in tiles:
                        add_up("gate", h, t)
                    if h == 0:
                        quantise("up", 0)
                    if h + 1 < H_TILES:
                        for t in tiles:
                            adapter_matmul("up", h, t)
                    for t in tiles:
                        projection("up", h, t)
                    if h + 1 < H_TILES:
                        for side in sides:
                            scalar_share(side, h + 1)
                    else:
                        for t in tiles:
                            adapter_out("up", h, t)
                    if h + 1 == H_TILES:
                        for t in range(T_TILES // 2):
                            silu(h, t, 1)
